import numpy as np
import ml_dtypes


def mxq(x, axis, fmt="e4m3"):
    dtype, down = {"e4m3": (ml_dtypes.float8_e4m3fn, 7), "e5m2": (ml_dtypes.float8_e5m2, 14)}[fmt]
    v = np.moveaxis(np.asarray(x, np.float32).astype(ml_dtypes.bfloat16).astype(np.float64), axis, -1)
    blocks = v.reshape(v.shape[:-1] + (-1, 32))
    amax = np.abs(blocks).max(-1, keepdims=True)
    byte = np.maximum(np.where(amax > 0, np.frexp(amax)[1] - 1 + 127, 0) - down, 1)
    scale = np.exp2(byte - 127.0)
    codes = (blocks / scale).astype(np.float32).astype(dtype).astype(np.float64)
    return np.moveaxis((codes * scale).reshape(v.shape), -1, axis)


WIDE = False


def mx_kscale(k):
    if not WIDE:
        return np.ones(k)
    levels = np.array([10, -10, 5, -5, 0])
    a = np.random.permutation(np.resize(levels, k // 512 * 4)).reshape(k // 512, 4)
    idx = np.arange(k)
    return np.exp2(a[idx // 512, idx % 128 // 32])


BF16 = ml_dtypes.bfloat16


def bf(x):
    return np.asarray(x, np.float32).astype(BF16)


def f64(x):
    return np.asarray(x).astype(np.float64)


E2M1 = np.array([0.0, 0.5, 1.0, 1.5, 2.0, 3.0, 4.0, 6.0, -0.0, -0.5, -1.0, -1.5, -2.0, -3.0, -4.0, -6.0])


def pack_weight(w, fmt):
    k, n = w.shape
    w = f64(bf(w)).reshape(k // 32, 32, n)
    amax = np.abs(w).max(1)
    if fmt == "e4m3":
        byte = np.frexp(amax)[1] - 1 + 127 - 7
    else:
        mant, ex = np.frexp(amax / 6.0)
        byte = np.where(mant > 0.5, ex, ex - 1) + 127
    byte = np.clip(np.where(amax > 0, byte, 1), 1, 254)
    scaled = (w * np.exp2(127.0 - byte)[:, None, :]).reshape(k, n).astype(np.float32)
    by_word = np.ascontiguousarray(scaled.reshape(k // 512, 128, 4, n).transpose(0, 1, 3, 2))
    if fmt == "e4m3":
        words = by_word.astype(ml_dtypes.float8_e4m3fn).view(np.uint8)
    else:
        c = by_word.astype(ml_dtypes.float4_e2m1fn).view(np.uint8) & 0xF
        words = c[..., 0::2] | (c[..., 1::2] << 4)
    return np.ascontiguousarray(words), np.ascontiguousarray(byte.astype(np.uint8).reshape(k // 512, 16, n))


def unpack_weight(words, scales, fmt):
    g, p, n, _ = words.shape
    if fmt == "e4m3":
        vals = np.ascontiguousarray(words).view(ml_dtypes.float8_e4m3fn).astype(np.float64)
    else:
        nib = np.empty((g, p, n, 4), np.uint8)
        nib[..., 0::2] = words & 0xF
        nib[..., 1::2] = words >> 4
        vals = E2M1[nib]
    vals = vals * np.repeat(np.exp2(scales.astype(np.float64) - 127.0), 8, axis=1)[..., None]
    return vals.transpose(0, 1, 3, 2).reshape(g * 512, n)


B, I, H = 8192, 1024, 128
G = 4
MXH = H % 512 == 0


def sigmoid(v):
    return 1.0 / (1.0 + np.exp(-v))


def setup_inputs():
    s = mx_kscale(I)
    t = mx_kscale(H) if MXH else np.ones(H)
    x = bf(np.random.standard_normal((B, I)) * s)
    h = bf(np.random.standard_normal((B, H)) * t)
    c = bf(np.random.standard_normal((B, H)))
    wx = np.random.standard_normal((G, H, I)) * 0.8 / np.sqrt(I) / s
    cat = np.ascontiguousarray(wx.swapaxes(1, 2)).reshape(-1, H)
    Wx_words, Wx_scales = pack_weight(cat, "e4m3")
    Wh = bf(np.random.standard_normal((4, H, H)) * 0.8 / np.sqrt(H) / t)
    bx = bf(np.random.standard_normal((4, H)) * 0.3)
    bh = bf(np.random.standard_normal((4, H)) * 0.3)
    return {"x": x, "h": h, "c": c, "Wx_words": Wx_words, "Wx_scales": Wx_scales,
            "Wh": Wh, "bx": bx, "bh": bh}


def reference(x, h, c, Wx_words, Wx_scales, Wh, bx, bh):
    wx = unpack_weight(Wx_words, Wx_scales, "e4m3").reshape(G, I, H).swapaxes(1, 2).reshape(G * H, I)
    wh = f64(Wh).reshape(4 * H, H)
    gx = (mxq(f64(x), 1, "e4m3") @ wx.T) + f64(bx).reshape(-1)
    if MXH:
        gh = (mxq(f64(h), 1, "e4m3") @ mxq(wh, 1, "e4m3").T) + f64(bh).reshape(-1)
    else:
        gh = f64(h) @ wh.T + f64(bh).reshape(-1)
    g = (gx + gh).reshape(-1, 4, H)
    i = sigmoid(g[:, 0])
    f = sigmoid(g[:, 1])
    gc = np.tanh(g[:, 2])
    o = sigmoid(g[:, 3])
    c_new = f * f64(c) + i * gc
    hs = o * np.tanh(c_new)
    return (hs, c_new)

@@ -1,0 +1,254 @@
+from contextlib import ExitStack
+
+import concourse.mybir as mybir
+from concourse.masks import make_identity
+
+F32 = mybir.dt.float32
+BF16 = mybir.dt.bfloat16
+I32 = mybir.dt.int32
+U32 = mybir.dt.uint32
+U8 = mybir.dt.uint8
+FP8X4 = mybir.dt.float8_e4m3fn_x4
+ACT = mybir.ActivationFunctionType
+ALU = mybir.AluOpType
+
+P = 128
+BATCH, FEATURES, HIDDEN, GATES = 8192, 1024, 128, 4
+GATE_COLS = GATES * HIDDEN
+K_PASS = 4 * P
+PASSES = FEATURES // K_PASS
+WORDS_PASS = K_PASS // 2
+TILES = BATCH // P
+ROUND = 2
+ROUNDS = TILES // ROUND
+GROUP = 4
+GROUPS = TILES // GROUP
+ROUNDS_PER_GROUP = GROUP // ROUND
+LOADS_AHEAD = 3
+ROUNDS_AHEAD = 2
+
+FLOPS = 2 * BATCH * (FEATURES + HIDDEN) * GATE_COLS
+
+
+def tile_lstmcell_t_e_kernel(tc, x, h, c, Wx_words, Wx_scales, Wh, bx, bh, out_0, out_1):
+    nc = tc.nc
+
+    x_rows = x.rearrange("(p t) k -> p t k", t=TILES)
+    h_rows = h.rearrange("(p t) k -> p t k", t=TILES)
+    c_rows = c.rearrange("(p t) n -> p t n", t=TILES)
+    hs_rows = out_0.rearrange("(p t) n -> p t n", t=TILES)
+    cell_rows = out_1.rearrange("(p t) n -> p t n", t=TILES)
+
+    with ExitStack() as ctx:
+        consts = ctx.enter_context(tc.tile_pool(name="consts", bufs=1))
+        loads = ctx.enter_context(tc.tile_pool(name="loads", bufs=LOADS_AHEAD + 1))
+        staged = ctx.enter_context(tc.tile_pool(name="staged", bufs=2))
+        packed = ctx.enter_context(tc.tile_pool(name="packed", bufs=ROUNDS_AHEAD + 2))
+        gates = ctx.enter_context(tc.tile_pool(name="gates", bufs=3))
+        cells = ctx.enter_context(tc.tile_pool(name="cells", bufs=4))
+        psum_x = ctx.enter_context(tc.psum_pool(name="psum_x", bufs=3))
+        psum_h = ctx.enter_context(tc.psum_pool(name="psum_h", bufs=1))
+        psum_g = ctx.enter_context(tc.psum_pool(name="psum_g", bufs=4))
+        ctx.enter_context(tc.manual_schedule())
+
+        live = {}
+
+        def load_x_h(s):
+            tiles_of_s = slice(s * GROUP, (s + 1) * GROUP)
+            x_sb = loads.tile([P, GROUP, FEATURES], BF16)
+            nc.sync.dma_start(out=x_sb[:], in_=x_rows[:, tiles_of_s, :])
+            h_sb = loads.tile([P, GROUP, HIDDEN], BF16)
+            nc.sync.dma_start(out=h_sb[:], in_=h_rows[:, tiles_of_s, :])
+            live["x", s] = x_sb
+            live["h", s] = h_sb
+
+        def load_c(s):
+            c_sb = cells.tile([P, GROUP, HIDDEN], BF16)
+            nc.sync.dma_start(out=c_sb[:], in_=c_rows[:, s * GROUP : (s + 1) * GROUP, :])
+            live["c", s] = c_sb
+
+        load_x_h(0)
+        load_x_h(1)
+
+        w_codes = consts.tile([P, PASSES, GATE_COLS], U32, align_bytes=64)
+        code_words = (
+            Wx_words.rearrange("g p n t -> g p (n t)").bitcast(I32).rearrange("(e j) p n -> j p e n", j=PASSES)
+        )
+        for j in range(PASSES):
+            nc.sync.dma_start(
+                out=w_codes[:, j, :].bitcast(I32).rearrange("p (e n) -> p e n", e=GATES), in_=code_words[j]
+            )
+        w_scales = consts.tile([P, PASSES, GATE_COLS], U8, align_bytes=64)
+        nc.vector.memset(w_scales[:].bitcast(I32), 0)
+        scale_rows = Wx_scales.bitcast(I32).rearrange("(e j) q n -> j q e n", j=PASSES)
+        for j in range(PASSES):
+            for quadrant in range(4):
+                nc.sync.dma_start(
+                    out=w_scales[32 * quadrant : 32 * quadrant + 4, j, :]
+                    .bitcast(I32)
+                    .rearrange("q (e n) -> q e n", e=GATES),
+                    in_=scale_rows[j, 4 * quadrant : 4 * quadrant + 4],
+                )
+        for s in range(2, LOADS_AHEAD):
+            load_x_h(s)
+
+        wh_sb = consts.tile([P, GATES, HIDDEN], BF16)
+        nc.scalar.dma_start(out=wh_sb[:], in_=Wh.rearrange("e n k -> n e k"))
+        bias_rows = consts.tile([P, GATE_COLS], BF16)
+        nc.vector.memset(bias_rows[:], 0.0)
+        nc.scalar.dma_start(out=bias_rows[0:1, :], in_=bx.rearrange("(o e) n -> o (e n)", o=1))
+        nc.scalar.dma_start(out=bias_rows[1:2, :], in_=bh.rearrange("(o e) n -> o (e n)", o=1))
+        ones = consts.tile([P, P], BF16)
+        nc.vector.memset(ones[:], 1.0)
+        warm = consts.tile([P, 1], F32)
+        nc.vector.memset(warm[:], 0.0)
+        nc.scalar.activation(out=warm[:], in_=warm[:], func=ACT.Sigmoid)
+
+        ident_bf = consts.tile([P, P], BF16)
+        make_identity(nc, ident_bf[:])
+        ident_f32 = consts.tile([P, P], F32)
+        make_identity(nc, ident_f32[:])
+
+        whT_ps = psum_h.tile([P, GATES, HIDDEN], BF16, tag="hT")
+        for e in range(GATES):
+            nc.tensor.transpose(out=whT_ps[:, e, :], in_=wh_sb[:, e, :], identity=ident_bf[:])
+        whT = consts.tile([P, GATE_COLS], BF16)
+        nc.vector.tensor_copy(out=whT[:], in_=whT_ps[:].rearrange("k e n -> k (e n)"))
+        bias_ps = psum_g.tile([P, GATE_COLS], F32, tag="product")
+        nc.tensor.matmul(out=bias_ps[:], lhsT=ones[:], rhs=bias_rows[:], start=True, stop=True)
+        bias = consts.tile([P, GATE_COLS], F32)
+        nc.vector.tensor_copy(out=bias[:], in_=bias_ps[:])
+
+        def tiles_of_round(r):
+            return [(t, t // GROUP, t % GROUP) for t in range(r * ROUND, (r + 1) * ROUND)]
+
+        def transpose_x_h(r):
+            for t, group, place in tiles_of_round(r):
+                x_words = live["x", group][:].bitcast(F32)
+                xT_ps = psum_x.tile([P, 2 * PASSES, P], F32)
+                for j in range(PASSES):
+                    for u in range(2):
+                        nc.tensor.transpose(
+                            out=xT_ps[:, 2 * j + u, :],
+                            in_=x_words[:, place, WORDS_PASS * j + u : WORDS_PASS * (j + 1) : 2],
+                            identity=ident_f32[:],
+                        )
+                live["xT_ps", t] = xT_ps
+            hT_ps = psum_h.tile([P, ROUND, P], BF16, tag="hT")
+            for t, group, place in tiles_of_round(r):
+                nc.tensor.transpose(out=hT_ps[:, t % ROUND, :], in_=live["h", group][:, place, :], identity=ident_bf[:])
+            live["hT_ps", r] = hT_ps
+
+        def copy_transposes(r):
+            x_grouped = staged.tile([P, ROUND * FEATURES], BF16, align_bytes=64)
+            grouped_words = x_grouped[:].bitcast(F32).rearrange(
+                "p (t j r u) -> p t j r u", t=ROUND, j=PASSES, u=2
+            )
+            for t, group, place in tiles_of_round(r):
+                nc.scalar.copy(
+                    out=grouped_words[:, t % ROUND],
+                    in_=live["xT_ps", t][:].rearrange("p (j u) r -> p j r u", u=2),
+                )
+            hT = packed.tile([P, ROUND, P], BF16)
+            nc.scalar.copy(out=hT[:], in_=live["hT_ps", r][:])
+            live["x_grouped", r] = x_grouped
+            live["hT", r] = hT
+
+        def quantise_x(r):
+            x_codes = packed.tile([P, ROUND * PASSES * P], U32, align_bytes=64)
+            x_scales = packed.tile([P, ROUND * PASSES * P], U8, align_bytes=64)
+            nc.vector.quantize_mx(out=x_codes[:].bitcast(FP8X4), scales=x_scales[:], in_=live["x_grouped", r][:])
+            live["x_codes", r] = x_codes
+            live["x_scales", r] = x_scales
+
+        def products_and_sums(r):
+            g_sb = gates.tile([P, ROUND, GATE_COLS], F32)
+            for i in range(ROUND):
+                gh_ps = psum_g.tile([P, GATE_COLS], F32, tag="product")
+                nc.tensor.matmul(out=gh_ps[:], lhsT=live["hT", r][:, i, :], rhs=whT[:], start=True, stop=True)
+                gx_ps = psum_g.tile([P, GATE_COLS], F32, tag="product")
+                for j in range(PASSES):
+                    rows = slice((i * PASSES + j) * P, (i * PASSES + j + 1) * P)
+                    nc.tensor.matmul_mx(
+                        out=gx_ps[:],
+                        lhsT=live["x_codes", r][:, rows].bitcast(FP8X4),
+                        lhsT_scale=live["x_scales", r][:, rows],
+                        rhs=w_codes[:, j, :].bitcast(FP8X4),
+                        rhs_scale=w_scales[:, j, :],
+                        start=(j == 0),
+                        stop=(j == PASSES - 1),
+                    )
+                nc.vector.tensor_tensor(out=g_sb[:, i, :], in0=gh_ps[:], in1=bias[:], op=ALU.add)
+                nc.vector.tensor_tensor(out=g_sb[:, i, :], in0=gx_ps[:], in1=g_sb[:, i, :], op=ALU.add)
+            live["g", r] = g_sb
+
+        def gate_functions(r):
+            group = r // ROUNDS_PER_GROUP
+            if r % ROUNDS_PER_GROUP == 0:
+                act_new = cells.tile([P, GROUP, GATE_COLS], F32, tag="act")
+                live["act", group] = act_new
+            first = (r % ROUNDS_PER_GROUP) * ROUND
+            act = live["act", group][:, first : first + ROUND, :]
+            g_sb = live["g", r]
+            i_f = slice(0, 2 * HIDDEN)
+            g_ = slice(2 * HIDDEN, 3 * HIDDEN)
+            o_ = slice(3 * HIDDEN, 4 * HIDDEN)
+            nc.scalar.activation(out=act[:, :, i_f], in_=g_sb[:, :, i_f], func=ACT.Sigmoid)
+            nc.scalar.activation(out=act[:, :, g_], in_=g_sb[:, :, g_], func=ACT.Tanh)
+            nc.scalar.activation(out=act[:, :, o_], in_=g_sb[:, :, o_], func=ACT.Sigmoid)
+
+        def cell_engine(group):
+            return nc.vector if group == GROUPS - 1 else nc.gpsimd
+
+        def new_cell(group):
+            act = live["act", group]
+            engine = cell_engine(group)
+            f_c = cells.tile([P, GROUP, HIDDEN], F32)
+            engine.tensor_tensor(out=f_c[:], in0=act[:, :, HIDDEN : 2 * HIDDEN], in1=live["c", group][:], op=ALU.mult)
+            i_g = cells.tile([P, GROUP, HIDDEN], F32)
+            engine.tensor_tensor(
+                out=i_g[:], in0=act[:, :, 0:HIDDEN], in1=act[:, :, 2 * HIDDEN : 3 * HIDDEN], op=ALU.mult
+            )
+            c_new = cells.tile([P, GROUP, HIDDEN], F32)
+            engine.tensor_tensor(out=c_new[:], in0=f_c[:], in1=i_g[:], op=ALU.add)
+            live["c_new", group] = c_new
+
+        def tanh_of_cell(group):
+            tanh_c = cells.tile([P, GROUP, HIDDEN], F32)
+            nc.scalar.activation(out=tanh_c[:], in_=live["c_new", group][:], func=ACT.Tanh)
+            live["tanh_c", group] = tanh_c
+
+        def hidden_and_stores(group):
+            hs = cells.tile([P, GROUP, HIDDEN], F32)
+            cell_engine(group).tensor_tensor(
+                out=hs[:], in0=live["act", group][:, :, 3 * HIDDEN : 4 * HIDDEN], in1=live["tanh_c", group][:], op=ALU.mult
+            )
+            tiles_of_group = slice(group * GROUP, (group + 1) * GROUP)
+            nc.sync.dma_start(out=cell_rows[:, tiles_of_group, :], in_=live["c_new", group][:])
+            nc.sync.dma_start(out=hs_rows[:, tiles_of_group, :], in_=hs[:])
+
+        for step in range(-ROUNDS_AHEAD, ROUNDS + ROUNDS_PER_GROUP + 1):
+            ahead = step + ROUNDS_AHEAD
+            if ahead < ROUNDS:
+                next_load = ahead // ROUNDS_PER_GROUP + LOADS_AHEAD
+                if ahead % ROUNDS_PER_GROUP == 0 and next_load < GROUPS:
+                    load_x_h(next_load)
+                transpose_x_h(ahead)
+                copy_transposes(ahead)
+            if 0 <= step < ROUNDS:
+                if step % ROUNDS_PER_GROUP == 0:
+                    load_c(step // ROUNDS_PER_GROUP)
+                products_and_sums(step)
+            if ahead < ROUNDS:
+                quantise_x(ahead)
+            behind = step - 1
+            if 0 <= behind < ROUNDS:
+                gate_functions(behind)
+            if behind >= 0 and behind % ROUNDS_PER_GROUP == ROUNDS_PER_GROUP - 1:
+                group = behind // ROUNDS_PER_GROUP
+                if group >= 1:
+                    tanh_of_cell(group - 1)
+                if group < GROUPS:
+                    new_cell(group)
+                if group >= 1:
+                    hidden_and_stores(group - 1)

@@ -134,10 +134,12 @@ def tile_lstmcell_t_e_kernel(tc, x, h, c, Wx_words, Wx_scales, Wh, bx, bh, out_0
                             identity=ident_f32[:],
                         )
                 live["xT_ps", t] = xT_ps
-            hT_ps = psum_h.tile([P, ROUND, P], BF16, tag="hT")
-            for t, group, place in tiles_of_round(r):
-                nc.tensor.transpose(out=hT_ps[:, t % ROUND, :], in_=live["h", group][:, place, :], identity=ident_bf[:])
-            live["hT_ps", r] = hT_ps
+            if r % ROUNDS_PER_GROUP == 0:
+                group = r // ROUNDS_PER_GROUP
+                hT_ps = psum_h.tile([P, GROUP, P], BF16, tag="hT")
+                for place in range(GROUP):
+                    nc.tensor.transpose(out=hT_ps[:, place, :], in_=live["h", group][:, place, :], identity=ident_bf[:])
+                live["hT_ps", group] = hT_ps
 
         def copy_transposes(r):
             x_grouped = staged.tile([P, ROUND * FEATURES], BF16, align_bytes=64)
@@ -149,10 +151,12 @@ def tile_lstmcell_t_e_kernel(tc, x, h, c, Wx_words, Wx_scales, Wh, bx, bh, out_0
                     out=grouped_words[:, t % ROUND],
                     in_=live["xT_ps", t][:].rearrange("p (j u) r -> p j r u", u=2),
                 )
-            hT = packed.tile([P, ROUND, P], BF16)
-            nc.scalar.copy(out=hT[:], in_=live["hT_ps", r][:])
             live["x_grouped", r] = x_grouped
-            live["hT", r] = hT
+            if r % ROUNDS_PER_GROUP == 0:
+                group = r // ROUNDS_PER_GROUP
+                hT = packed.tile([P, GROUP, P], BF16)
+                nc.scalar.copy(out=hT[:], in_=live["hT_ps", group][:])
+                live["hT", group] = hT
 
         def quantise_x(r):
             x_codes = packed.tile([P, ROUND * PASSES * P], U32, align_bytes=64)
@@ -162,10 +166,19 @@ def tile_lstmcell_t_e_kernel(tc, x, h, c, Wx_words, Wx_scales, Wh, bx, bh, out_0
             live["x_scales", r] = x_scales
 
         def products_and_sums(r):
-            g_sb = gates.tile([P, ROUND, GATE_COLS], F32)
-            for i in range(ROUND):
+            group = r // ROUNDS_PER_GROUP
+            if r % ROUNDS_PER_GROUP == 0:
+                g_new = gates.tile([P, GROUP, GATE_COLS], F32, tag="g")
+                live["g", group] = g_new
+            places = range((r % ROUNDS_PER_GROUP) * ROUND, (r % ROUNDS_PER_GROUP + 1) * ROUND)
+            g_sb = live["g", group]
+            gh_banks = {}
+            gx_banks = {}
+            for place in places:
                 gh_ps = psum_g.tile([P, GATE_COLS], F32, tag="product")
-                nc.tensor.matmul(out=gh_ps[:], lhsT=live["hT", r][:, i, :], rhs=whT[:], start=True, stop=True)
+                nc.tensor.matmul(out=gh_ps[:], lhsT=live["hT", group][:, place, :], rhs=whT[:], start=True, stop=True)
+                gh_banks[place] = gh_ps
+            for i, place in enumerate(places):
                 gx_ps = psum_g.tile([P, GATE_COLS], F32, tag="product")
                 for j in range(PASSES):
                     rows = slice((i * PASSES + j) * P, (i * PASSES + j + 1) * P)
@@ -178,18 +191,16 @@ def tile_lstmcell_t_e_kernel(tc, x, h, c, Wx_words, Wx_scales, Wh, bx, bh, out_0
                         start=(j == 0),
                         stop=(j == PASSES - 1),
                     )
-                nc.vector.tensor_tensor(out=g_sb[:, i, :], in0=gh_ps[:], in1=bias[:], op=ALU.add)
-                nc.vector.tensor_tensor(out=g_sb[:, i, :], in0=gx_ps[:], in1=g_sb[:, i, :], op=ALU.add)
-            live["g", r] = g_sb
+                gx_banks[place] = gx_ps
+            for place in places:
+                nc.vector.tensor_tensor(out=g_sb[:, place, :], in0=gh_banks[place][:], in1=bias[:], op=ALU.add)
+            for place in places:
+                nc.vector.tensor_tensor(out=g_sb[:, place, :], in0=gx_banks[place][:], in1=g_sb[:, place, :], op=ALU.add)
 
-        def gate_functions(r):
-            group = r // ROUNDS_PER_GROUP
-            if r % ROUNDS_PER_GROUP == 0:
-                act_new = cells.tile([P, GROUP, GATE_COLS], F32, tag="act")
-                live["act", group] = act_new
-            first = (r % ROUNDS_PER_GROUP) * ROUND
-            act = live["act", group][:, first : first + ROUND, :]
-            g_sb = live["g", r]
+        def gate_functions(group):
+            act = cells.tile([P, GROUP, GATE_COLS], F32)
+            live["act", group] = act
+            g_sb = live["g", group]
             i_f = slice(0, 2 * HIDDEN)
             g_ = slice(2 * HIDDEN, 3 * HIDDEN)
             o_ = slice(3 * HIDDEN, 4 * HIDDEN)
@@ -242,10 +253,10 @@ def tile_lstmcell_t_e_kernel(tc, x, h, c, Wx_words, Wx_scales, Wh, bx, bh, out_0
             if ahead < ROUNDS:
                 quantise_x(ahead)
             behind = step - 1
-            if 0 <= behind < ROUNDS:
-                gate_functions(behind)
             if behind >= 0 and behind % ROUNDS_PER_GROUP == ROUNDS_PER_GROUP - 1:
                 group = behind // ROUNDS_PER_GROUP
+                if group < GROUPS:
+                    gate_functions(group)
                 if group >= 1:
                     tanh_of_cell(group - 1)
                 if group < GROUPS:

@@ -56,9 +56,14 @@ def tile_lstmcell_t_e_kernel(tc, x, h, c, Wx_words, Wx_scales, Wh, bx, bh, out_0
         def load_x_h(s):
             tiles_of_s = slice(s * GROUP, (s + 1) * GROUP)
             x_sb = loads.tile([P, GROUP, FEATURES], BF16)
-            nc.sync.dma_start(out=x_sb[:], in_=x_rows[:, tiles_of_s, :])
             h_sb = loads.tile([P, GROUP, HIDDEN], BF16)
-            nc.sync.dma_start(out=h_sb[:], in_=h_rows[:, tiles_of_s, :])
+            if s == 0:
+                nc.sync.dma_start(out=x_sb[:, 0:ROUND, :], in_=x_rows[:, 0:ROUND, :])
+                nc.sync.dma_start(out=h_sb[:], in_=h_rows[:, tiles_of_s, :])
+                nc.sync.dma_start(out=x_sb[:, ROUND:GROUP, :], in_=x_rows[:, ROUND:GROUP, :])
+            else:
+                nc.sync.dma_start(out=x_sb[:], in_=x_rows[:, tiles_of_s, :])
+                nc.sync.dma_start(out=h_sb[:], in_=h_rows[:, tiles_of_s, :])
             live["x", s] = x_sb
             live["h", s] = h_sb
 
@@ -197,48 +202,59 @@ def tile_lstmcell_t_e_kernel(tc, x, h, c, Wx_words, Wx_scales, Wh, bx, bh, out_0
             for place in places:
                 nc.vector.tensor_tensor(out=g_sb[:, place, :], in0=gx_banks[place][:], in1=g_sb[:, place, :], op=ALU.add)
 
-        def gate_functions(group):
-            act = cells.tile([P, GROUP, GATE_COLS], F32)
-            live["act", group] = act
+        WHOLE = slice(0, GROUP)
+
+        def tile_of_group(name, group, columns):
+            if (name, group) not in live:
+                fresh = cells.tile([P, GROUP, columns], F32, tag=name)
+                live[name, group] = fresh
+            return live[name, group]
+
+        def gate_functions(group, part=WHOLE):
+            act = tile_of_group("act", group, GATE_COLS)
             g_sb = live["g", group]
             i_f = slice(0, 2 * HIDDEN)
             g_ = slice(2 * HIDDEN, 3 * HIDDEN)
             o_ = slice(3 * HIDDEN, 4 * HIDDEN)
-            nc.scalar.activation(out=act[:, :, i_f], in_=g_sb[:, :, i_f], func=ACT.Sigmoid)
-            nc.scalar.activation(out=act[:, :, g_], in_=g_sb[:, :, g_], func=ACT.Tanh)
-            nc.scalar.activation(out=act[:, :, o_], in_=g_sb[:, :, o_], func=ACT.Sigmoid)
+            nc.scalar.activation(out=act[:, part, i_f], in_=g_sb[:, part, i_f], func=ACT.Sigmoid)
+            nc.scalar.activation(out=act[:, part, g_], in_=g_sb[:, part, g_], func=ACT.Tanh)
+            nc.scalar.activation(out=act[:, part, o_], in_=g_sb[:, part, o_], func=ACT.Sigmoid)
 
         def cell_engine(group):
             return nc.vector if group == GROUPS - 1 else nc.gpsimd
 
-        def new_cell(group):
+        def new_cell(group, part=WHOLE):
             act = live["act", group]
             engine = cell_engine(group)
-            f_c = cells.tile([P, GROUP, HIDDEN], F32)
-            engine.tensor_tensor(out=f_c[:], in0=act[:, :, HIDDEN : 2 * HIDDEN], in1=live["c", group][:], op=ALU.mult)
-            i_g = cells.tile([P, GROUP, HIDDEN], F32)
+            f_c = tile_of_group("f_c", group, HIDDEN)
             engine.tensor_tensor(
-                out=i_g[:], in0=act[:, :, 0:HIDDEN], in1=act[:, :, 2 * HIDDEN : 3 * HIDDEN], op=ALU.mult
+                out=f_c[:, part], in0=act[:, part, HIDDEN : 2 * HIDDEN], in1=live["c", group][:, part], op=ALU.mult
             )
-            c_new = cells.tile([P, GROUP, HIDDEN], F32)
-            engine.tensor_tensor(out=c_new[:], in0=f_c[:], in1=i_g[:], op=ALU.add)
-            live["c_new", group] = c_new
-
-        def tanh_of_cell(group):
-            tanh_c = cells.tile([P, GROUP, HIDDEN], F32)
-            nc.scalar.activation(out=tanh_c[:], in_=live["c_new", group][:], func=ACT.Tanh)
-            live["tanh_c", group] = tanh_c
-
-        def hidden_and_stores(group):
-            hs = cells.tile([P, GROUP, HIDDEN], F32)
-            cell_engine(group).tensor_tensor(
-                out=hs[:], in0=live["act", group][:, :, 3 * HIDDEN : 4 * HIDDEN], in1=live["tanh_c", group][:], op=ALU.mult
+            i_g = tile_of_group("i_g", group, HIDDEN)
+            engine.tensor_tensor(
+                out=i_g[:, part], in0=act[:, part, 0:HIDDEN], in1=act[:, part, 2 * HIDDEN : 3 * HIDDEN], op=ALU.mult
             )
-            tiles_of_group = slice(group * GROUP, (group + 1) * GROUP)
-            nc.sync.dma_start(out=cell_rows[:, tiles_of_group, :], in_=live["c_new", group][:])
-            nc.sync.dma_start(out=hs_rows[:, tiles_of_group, :], in_=hs[:])
+            c_new = tile_of_group("c_new", group, HIDDEN)
+            engine.tensor_tensor(out=c_new[:, part], in0=f_c[:, part], in1=i_g[:, part], op=ALU.add)
 
-        for step in range(-ROUNDS_AHEAD, ROUNDS + ROUNDS_PER_GROUP + 1):
+        def tanh_of_cell(group, part=WHOLE):
+            tanh_c = tile_of_group("tanh_c", group, HIDDEN)
+            nc.scalar.activation(out=tanh_c[:, part], in_=live["c_new", group][:, part], func=ACT.Tanh)
+
+        def hidden_and_stores(group, part=WHOLE, engine=None):
+            hs = tile_of_group("hs", group, HIDDEN)
+            (engine or cell_engine(group)).tensor_tensor(
+                out=hs[:, part],
+                in0=live["act", group][:, part, 3 * HIDDEN : 4 * HIDDEN],
+                in1=live["tanh_c", group][:, part],
+                op=ALU.mult,
+            )
+            tiles_of_part = slice(group * GROUP + part.start, group * GROUP + part.stop)
+            nc.sync.dma_start(out=cell_rows[:, tiles_of_part, :], in_=live["c_new", group][:, part])
+            nc.sync.dma_start(out=hs_rows[:, tiles_of_part, :], in_=hs[:, part])
+
+        LAST = GROUPS - 1
+        for step in range(-ROUNDS_AHEAD, ROUNDS):
             ahead = step + ROUNDS_AHEAD
             if ahead < ROUNDS:
                 next_load = ahead // ROUNDS_PER_GROUP + LOADS_AHEAD
@@ -255,11 +271,21 @@ def tile_lstmcell_t_e_kernel(tc, x, h, c, Wx_words, Wx_scales, Wh, bx, bh, out_0
             behind = step - 1
             if behind >= 0 and behind % ROUNDS_PER_GROUP == ROUNDS_PER_GROUP - 1:
                 group = behind // ROUNDS_PER_GROUP
-                if group < GROUPS:
-                    gate_functions(group)
+                gate_functions(group)
                 if group >= 1:
                     tanh_of_cell(group - 1)
-                if group < GROUPS:
-                    new_cell(group)
+                new_cell(group)
                 if group >= 1:
                     hidden_and_stores(group - 1)
+        first_half = slice(0, ROUND)
+        second_half = slice(ROUND, GROUP)
+        gate_functions(LAST, first_half)
+        new_cell(LAST, first_half)
+        gate_functions(LAST, second_half)
+        tanh_of_cell(LAST, first_half)
+        new_cell(LAST, second_half)
+        tanh_of_cell(LAST - 1)
+        hidden_and_stores(LAST, first_half)
+        tanh_of_cell(LAST, second_half)
+        hidden_and_stores(LAST - 1, engine=nc.vector)
+        hidden_and_stores(LAST, second_half)

@@ -114,15 +114,19 @@ def tile_lstmcell_t_e_kernel(tc, x, h, c, Wx_words, Wx_scales, Wh, bx, bh, out_0
         ident_f32 = consts.tile([P, P], F32)
         make_identity(nc, ident_f32[:])
 
-        whT_ps = psum_h.tile([P, GATES, HIDDEN], BF16, tag="hT")
-        for e in range(GATES):
-            nc.tensor.transpose(out=whT_ps[:, e, :], in_=wh_sb[:, e, :], identity=ident_bf[:])
         whT = consts.tile([P, GATE_COLS], BF16)
-        nc.vector.tensor_copy(out=whT[:], in_=whT_ps[:].rearrange("k e n -> k (e n)"))
-        bias_ps = psum_g.tile([P, GATE_COLS], F32, tag="product")
-        nc.tensor.matmul(out=bias_ps[:], lhsT=ones[:], rhs=bias_rows[:], start=True, stop=True)
         bias = consts.tile([P, GATE_COLS], F32)
-        nc.vector.tensor_copy(out=bias[:], in_=bias_ps[:])
+
+        def prepare_wh():
+            whT_ps = psum_g.tile([P, GATES, HIDDEN], BF16, tag="product")
+            for e in range(GATES):
+                nc.tensor.transpose(out=whT_ps[:, e, :], in_=wh_sb[:, e, :], identity=ident_bf[:])
+            nc.vector.tensor_copy(out=whT[:], in_=whT_ps[:].rearrange("k e n -> k (e n)"))
+
+        def prepare_bias():
+            bias_ps = psum_g.tile([P, GATE_COLS], F32, tag="product")
+            nc.tensor.matmul(out=bias_ps[:], lhsT=ones[:], rhs=bias_rows[:], start=True, stop=True)
+            nc.vector.tensor_copy(out=bias[:], in_=bias_ps[:])
 
         def tiles_of_round(r):
             return [(t, t // GROUP, t % GROUP) for t in range(r * ROUND, (r + 1) * ROUND)]
@@ -262,6 +266,10 @@ def tile_lstmcell_t_e_kernel(tc, x, h, c, Wx_words, Wx_scales, Wh, bx, bh, out_0
                     load_x_h(next_load)
                 transpose_x_h(ahead)
                 copy_transposes(ahead)
+            if step == -1:
+                prepare_wh()
+            if step == 0:
+                prepare_bias()
             if 0 <= step < ROUNDS:
                 if step % ROUNDS_PER_GROUP == 0:
                     load_c(step // ROUNDS_PER_GROUP)

@@ -185,7 +185,11 @@ def tile_lstmcell_t_e_kernel(tc, x, h, c, Wx_words, Wx_scales, Wh, bx, bh, out_0
             gx_banks = {}
             for place in places:
                 gh_ps = psum_g.tile([P, GATE_COLS], F32, tag="product")
-                nc.tensor.matmul(out=gh_ps[:], lhsT=live["hT", group][:, place, :], rhs=whT[:], start=True, stop=True)
+                if place == GROUP - 1:
+                    nc.tensor.matmul(out=gh_ps[:], lhsT=ones[:], rhs=bias_rows[:], start=True, stop=False)
+                nc.tensor.matmul(
+                    out=gh_ps[:], lhsT=live["hT", group][:, place, :], rhs=whT[:], start=not (place == GROUP - 1), stop=True
+                )
                 gh_banks[place] = gh_ps
             for i, place in enumerate(places):
                 gx_ps = psum_g.tile([P, GATE_COLS], F32, tag="product")
@@ -202,7 +206,10 @@ def tile_lstmcell_t_e_kernel(tc, x, h, c, Wx_words, Wx_scales, Wh, bx, bh, out_0
                     )
                 gx_banks[place] = gx_ps
             for place in places:
-                nc.vector.tensor_tensor(out=g_sb[:, place, :], in0=gh_banks[place][:], in1=bias[:], op=ALU.add)
+                if place == GROUP - 1:
+                    nc.scalar.copy(out=g_sb[:, place, :], in_=gh_banks[place][:])
+                else:
+                    nc.vector.tensor_tensor(out=g_sb[:, place, :], in0=gh_banks[place][:], in1=bias[:], op=ALU.add)
             for place in places:
                 nc.vector.tensor_tensor(out=g_sb[:, place, :], in0=gx_banks[place][:], in1=g_sb[:, place, :], op=ALU.add)
 

from contextlib import ExitStack

import concourse.mybir as mybir
from concourse.masks import make_identity

F32 = mybir.dt.float32
BF16 = mybir.dt.bfloat16
I32 = mybir.dt.int32
U32 = mybir.dt.uint32
U8 = mybir.dt.uint8
FP8X4 = mybir.dt.float8_e4m3fn_x4
ACT = mybir.ActivationFunctionType
ALU = mybir.AluOpType

P = 128
BATCH, FEATURES, HIDDEN, GATES = 8192, 1024, 128, 4
GATE_COLS = GATES * HIDDEN
K_PASS = 4 * P
PASSES = FEATURES // K_PASS
WORDS_PASS = K_PASS // 2
TILES = BATCH // P
ROUND = 2
ROUNDS = TILES // ROUND
GROUP = 4
GROUPS = TILES // GROUP
ROUNDS_PER_GROUP = GROUP // ROUND
LOADS_AHEAD = 3
ROUNDS_AHEAD = 2

FLOPS = 2 * BATCH * (FEATURES + HIDDEN) * GATE_COLS


def tile_lstmcell_t_e_kernel(tc, x, h, c, Wx_words, Wx_scales, Wh, bx, bh, out_0, out_1):
    nc = tc.nc

    x_rows = x.rearrange("(p t) k -> p t k", t=TILES)
    h_rows = h.rearrange("(p t) k -> p t k", t=TILES)
    c_rows = c.rearrange("(p t) n -> p t n", t=TILES)
    hs_rows = out_0.rearrange("(p t) n -> p t n", t=TILES)
    cell_rows = out_1.rearrange("(p t) n -> p t n", t=TILES)

    with ExitStack() as ctx:
        consts = ctx.enter_context(tc.tile_pool(name="consts", bufs=1))
        loads = ctx.enter_context(tc.tile_pool(name="loads", bufs=LOADS_AHEAD + 1))
        staged = ctx.enter_context(tc.tile_pool(name="staged", bufs=2))
        packed = ctx.enter_context(tc.tile_pool(name="packed", bufs=ROUNDS_AHEAD + 2))
        gates = ctx.enter_context(tc.tile_pool(name="gates", bufs=3))
        cells = ctx.enter_context(tc.tile_pool(name="cells", bufs=4))
        psum_x = ctx.enter_context(tc.psum_pool(name="psum_x", bufs=3))
        psum_h = ctx.enter_context(tc.psum_pool(name="psum_h", bufs=1))
        psum_g = ctx.enter_context(tc.psum_pool(name="psum_g", bufs=4))
        ctx.enter_context(tc.manual_schedule())

        live = {}

        def load_x_h(s):
            tiles_of_s = slice(s * GROUP, (s + 1) * GROUP)
            x_sb = loads.tile([P, GROUP, FEATURES], BF16)
            h_sb = loads.tile([P, GROUP, HIDDEN], BF16)
            if s == 0:
                nc.sync.dma_start(out=x_sb[:, 0:ROUND, :], in_=x_rows[:, 0:ROUND, :])
                nc.sync.dma_start(out=h_sb[:], in_=h_rows[:, tiles_of_s, :])
                nc.sync.dma_start(out=x_sb[:, ROUND:GROUP, :], in_=x_rows[:, ROUND:GROUP, :])
            else:
                nc.sync.dma_start(out=x_sb[:], in_=x_rows[:, tiles_of_s, :])
                nc.sync.dma_start(out=h_sb[:], in_=h_rows[:, tiles_of_s, :])
            live["x", s] = x_sb
            live["h", s] = h_sb

        def load_c(s):
            c_sb = cells.tile([P, GROUP, HIDDEN], BF16)
            nc.sync.dma_start(out=c_sb[:], in_=c_rows[:, s * GROUP : (s + 1) * GROUP, :])
            live["c", s] = c_sb

        load_x_h(0)
        load_x_h(1)

        w_codes = consts.tile([P, PASSES, GATE_COLS], U32, align_bytes=64)
        code_words = (
            Wx_words.rearrange("g p n t -> g p (n t)").bitcast(I32).rearrange("(e j) p n -> j p e n", j=PASSES)
        )
        for j in range(PASSES):
            nc.sync.dma_start(
                out=w_codes[:, j, :].bitcast(I32).rearrange("p (e n) -> p e n", e=GATES), in_=code_words[j]
            )
        w_scales = consts.tile([P, PASSES, GATE_COLS], U8, align_bytes=64)
        nc.vector.memset(w_scales[:].bitcast(I32), 0)
        scale_rows = Wx_scales.bitcast(I32).rearrange("(e j) q n -> j q e n", j=PASSES)
        for j in range(PASSES):
            for quadrant in range(4):
                nc.sync.dma_start(
                    out=w_scales[32 * quadrant : 32 * quadrant + 4, j, :]
                    .bitcast(I32)
                    .rearrange("q (e n) -> q e n", e=GATES),
                    in_=scale_rows[j, 4 * quadrant : 4 * quadrant + 4],
                )
        for s in range(2, LOADS_AHEAD):
            load_x_h(s)

        wh_sb = consts.tile([P, GATES, HIDDEN], BF16)
        nc.scalar.dma_start(out=wh_sb[:], in_=Wh.rearrange("e n k -> n e k"))
        bias_rows = consts.tile([P, GATE_COLS], BF16)
        nc.vector.memset(bias_rows[:], 0.0)
        nc.scalar.dma_start(out=bias_rows[0:1, :], in_=bx.rearrange("(o e) n -> o (e n)", o=1))
        nc.scalar.dma_start(out=bias_rows[1:2, :], in_=bh.rearrange("(o e) n -> o (e n)", o=1))
        ones = consts.tile([P, P], BF16)
        nc.vector.memset(ones[:], 1.0)
        warm = consts.tile([P, 1], F32)
        nc.vector.memset(warm[:], 0.0)
        nc.scalar.activation(out=warm[:], in_=warm[:], func=ACT.Sigmoid)

        ident_bf = consts.tile([P, P], BF16)
        make_identity(nc, ident_bf[:])
        ident_f32 = consts.tile([P, P], F32)
        make_identity(nc, ident_f32[:])

        whT = consts.tile([P, GATE_COLS], BF16)
        bias = consts.tile([P, GATE_COLS], F32)

        def prepare_wh():
            whT_ps = psum_g.tile([P, GATES, HIDDEN], BF16, tag="product")
            for e in range(GATES):
                nc.tensor.transpose(out=whT_ps[:, e, :], in_=wh_sb[:, e, :], identity=ident_bf[:])
            nc.vector.tensor_copy(out=whT[:], in_=whT_ps[:].rearrange("k e n -> k (e n)"))

        def prepare_bias():
            bias_ps = psum_g.tile([P, GATE_COLS], F32, tag="product")
            nc.tensor.matmul(out=bias_ps[:], lhsT=ones[:], rhs=bias_rows[:], start=True, stop=True)
            nc.vector.tensor_copy(out=bias[:], in_=bias_ps[:])

        def tiles_of_round(r):
            return [(t, t // GROUP, t % GROUP) for t in range(r * ROUND, (r + 1) * ROUND)]

        def transpose_x_h(r):
            for t, group, place in tiles_of_round(r):
                x_words = live["x", group][:].bitcast(F32)
                xT_ps = psum_x.tile([P, 2 * PASSES, P], F32)
                for j in range(PASSES):
                    for u in range(2):
                        nc.tensor.transpose(
                            out=xT_ps[:, 2 * j + u, :],
                            in_=x_words[:, place, WORDS_PASS * j + u : WORDS_PASS * (j + 1) : 2],
                            identity=ident_f32[:],
                        )
                live["xT_ps", t] = xT_ps
            if r % ROUNDS_PER_GROUP == 0:
                group = r // ROUNDS_PER_GROUP
                hT_ps = psum_h.tile([P, GROUP, P], BF16, tag="hT")
                for place in range(GROUP):
                    nc.tensor.transpose(out=hT_ps[:, place, :], in_=live["h", group][:, place, :], identity=ident_bf[:])
                live["hT_ps", group] = hT_ps

        def copy_transposes(r):
            x_grouped = staged.tile([P, ROUND * FEATURES], BF16, align_bytes=64)
            grouped_words = x_grouped[:].bitcast(F32).rearrange(
                "p (t j r u) -> p t j r u", t=ROUND, j=PASSES, u=2
            )
            for t, group, place in tiles_of_round(r):
                nc.scalar.copy(
                    out=grouped_words[:, t % ROUND],
                    in_=live["xT_ps", t][:].rearrange("p (j u) r -> p j r u", u=2),
                )
            live["x_grouped", r] = x_grouped
            if r % ROUNDS_PER_GROUP == 0:
                group = r // ROUNDS_PER_GROUP
                hT = packed.tile([P, GROUP, P], BF16)
                nc.scalar.copy(out=hT[:], in_=live["hT_ps", group][:])
                live["hT", group] = hT

        def quantise_x(r):
            x_codes = packed.tile([P, ROUND * PASSES * P], U32, align_bytes=64)
            x_scales = packed.tile([P, ROUND * PASSES * P], U8, align_bytes=64)
            nc.vector.quantize_mx(out=x_codes[:].bitcast(FP8X4), scales=x_scales[:], in_=live["x_grouped", r][:])
            live["x_codes", r] = x_codes
            live["x_scales", r] = x_scales

        def products_and_sums(r):
            group = r // ROUNDS_PER_GROUP
            if r % ROUNDS_PER_GROUP == 0:
                g_new = gates.tile([P, GROUP, GATE_COLS], F32, tag="g")
                live["g", group] = g_new
            places = range((r % ROUNDS_PER_GROUP) * ROUND, (r % ROUNDS_PER_GROUP + 1) * ROUND)
            g_sb = live["g", group]
            gh_banks = {}
            gx_banks = {}
            for place in places:
                gh_ps = psum_g.tile([P, GATE_COLS], F32, tag="product")
                if place == GROUP - 1:
                    nc.tensor.matmul(out=gh_ps[:], lhsT=ones[:], rhs=bias_rows[:], start=True, stop=False)
                nc.tensor.matmul(
                    out=gh_ps[:], lhsT=live["hT", group][:, place, :], rhs=whT[:], start=not (place == GROUP - 1), stop=True
                )
                gh_banks[place] = gh_ps
            for i, place in enumerate(places):
                gx_ps = psum_g.tile([P, GATE_COLS], F32, tag="product")
                for j in range(PASSES):
                    rows = slice((i * PASSES + j) * P, (i * PASSES + j + 1) * P)
                    nc.tensor.matmul_mx(
                        out=gx_ps[:],
                        lhsT=live["x_codes", r][:, rows].bitcast(FP8X4),
                        lhsT_scale=live["x_scales", r][:, rows],
                        rhs=w_codes[:, j, :].bitcast(FP8X4),
                        rhs_scale=w_scales[:, j, :],
                        start=(j == 0),
                        stop=(j == PASSES - 1),
                    )
                gx_banks[place] = gx_ps
            for place in places:
                if place == GROUP - 1:
                    nc.scalar.copy(out=g_sb[:, place, :], in_=gh_banks[place][:])
                else:
                    nc.vector.tensor_tensor(out=g_sb[:, place, :], in0=gh_banks[place][:], in1=bias[:], op=ALU.add)
            for place in places:
                nc.vector.tensor_tensor(out=g_sb[:, place, :], in0=gx_banks[place][:], in1=g_sb[:, place, :], op=ALU.add)

        WHOLE = slice(0, GROUP)

        def tile_of_group(name, group, columns):
            if (name, group) not in live:
                fresh = cells.tile([P, GROUP, columns], F32, tag=name)
                live[name, group] = fresh
            return live[name, group]

        def gate_functions(group, part=WHOLE):
            act = tile_of_group("act", group, GATE_COLS)
            g_sb = live["g", group]
            i_f = slice(0, 2 * HIDDEN)
            g_ = slice(2 * HIDDEN, 3 * HIDDEN)
            o_ = slice(3 * HIDDEN, 4 * HIDDEN)
            nc.scalar.activation(out=act[:, part, i_f], in_=g_sb[:, part, i_f], func=ACT.Sigmoid)
            nc.scalar.activation(out=act[:, part, g_], in_=g_sb[:, part, g_], func=ACT.Tanh)
            nc.scalar.activation(out=act[:, part, o_], in_=g_sb[:, part, o_], func=ACT.Sigmoid)

        def cell_engine(group):
            return nc.vector if group == GROUPS - 1 else nc.gpsimd

        def new_cell(group, part=WHOLE):
            act = live["act", group]
            engine = cell_engine(group)
            f_c = tile_of_group("f_c", group, HIDDEN)
            engine.tensor_tensor(
                out=f_c[:, part], in0=act[:, part, HIDDEN : 2 * HIDDEN], in1=live["c", group][:, part], op=ALU.mult
            )
            i_g = tile_of_group("i_g", group, HIDDEN)
            engine.tensor_tensor(
                out=i_g[:, part], in0=act[:, part, 0:HIDDEN], in1=act[:, part, 2 * HIDDEN : 3 * HIDDEN], op=ALU.mult
            )
            c_new = tile_of_group("c_new", group, HIDDEN)
            engine.tensor_tensor(out=c_new[:, part], in0=f_c[:, part], in1=i_g[:, part], op=ALU.add)

        def tanh_of_cell(group, part=WHOLE):
            tanh_c = tile_of_group("tanh_c", group, HIDDEN)
            nc.scalar.activation(out=tanh_c[:, part], in_=live["c_new", group][:, part], func=ACT.Tanh)

        def hidden_and_stores(group, part=WHOLE, engine=None):
            hs = tile_of_group("hs", group, HIDDEN)
            (engine or cell_engine(group)).tensor_tensor(
                out=hs[:, part],
                in0=live["act", group][:, part, 3 * HIDDEN : 4 * HIDDEN],
                in1=live["tanh_c", group][:, part],
                op=ALU.mult,
            )
            tiles_of_part = slice(group * GROUP + part.start, group * GROUP + part.stop)
            nc.sync.dma_start(out=cell_rows[:, tiles_of_part, :], in_=live["c_new", group][:, part])
            nc.sync.dma_start(out=hs_rows[:, tiles_of_part, :], in_=hs[:, part])

        LAST = GROUPS - 1
        for step in range(-ROUNDS_AHEAD, ROUNDS):
            ahead = step + ROUNDS_AHEAD
            if ahead < ROUNDS:
                next_load = ahead // ROUNDS_PER_GROUP + LOADS_AHEAD
                if ahead % ROUNDS_PER_GROUP == 0 and next_load < GROUPS:
                    load_x_h(next_load)
                transpose_x_h(ahead)
                copy_transposes(ahead)
            if step == -1:
                prepare_wh()
            if step == 0:
                prepare_bias()
            if 0 <= step < ROUNDS:
                if step % ROUNDS_PER_GROUP == 0:
                    load_c(step // ROUNDS_PER_GROUP)
                products_and_sums(step)
            if ahead < ROUNDS:
                quantise_x(ahead)
            behind = step - 1
            if behind >= 0 and behind % ROUNDS_PER_GROUP == ROUNDS_PER_GROUP - 1:
                group = behind // ROUNDS_PER_GROUP
                gate_functions(group)
                if group >= 1:
                    tanh_of_cell(group - 1)
                new_cell(group)
                if group >= 1:
                    hidden_and_stores(group - 1)
        first_half = slice(0, ROUND)
        second_half = slice(ROUND, GROUP)
        gate_functions(LAST, first_half)
        new_cell(LAST, first_half)
        gate_functions(LAST, second_half)
        tanh_of_cell(LAST, first_half)
        new_cell(LAST, second_half)
        tanh_of_cell(LAST - 1)
        hidden_and_stores(LAST, first_half)
        tanh_of_cell(LAST, second_half)
        hidden_and_stores(LAST - 1, engine=nc.vector)
        hidden_and_stores(LAST, second_half)
